import numpy as np
import ml_dtypes


def mxq(x, axis, fmt="e4m3"):
    dtype, down = {"e4m3": (ml_dtypes.float8_e4m3fn, 7), "e5m2": (ml_dtypes.float8_e5m2, 14)}[fmt]
    v = np.moveaxis(np.asarray(x, np.float32).astype(ml_dtypes.bfloat16).astype(np.float64), axis, -1)
    blocks = v.reshape(v.shape[:-1] + (-1, 32))
    amax = np.abs(blocks).max(-1, keepdims=True)
    byte = np.maximum(np.where(amax > 0, np.frexp(amax)[1] - 1 + 127, 0) - down, 1)
    scale = np.exp2(byte - 127.0)
    codes = (blocks / scale).astype(np.float32).astype(dtype).astype(np.float64)
    return np.moveaxis((codes * scale).reshape(v.shape), -1, axis)


WIDE = False


def mx_kscale(k):
    if not WIDE:
        return np.ones(k)
    levels = np.array([10, -10, 5, -5, 0])
    a = np.random.permutation(np.resize(levels, k // 512 * 4)).reshape(k // 512, 4)
    idx = np.arange(k)
    return np.exp2(a[idx // 512, idx % 128 // 32])


BF16 = ml_dtypes.bfloat16


def bf(x):
    return np.asarray(x, np.float32).astype(BF16)


def f64(x):
    return np.asarray(x).astype(np.float64)


B, D_IN, D_H = 512, 1024, 1024


def setup_inputs():
    s, t = mx_kscale(D_IN), mx_kscale(D_H)
    inp = {"x": bf(np.random.standard_normal((B, D_IN)) * s),
           "h_prev": bf(np.random.standard_normal((B, D_H)) * t),
           "c_prev": bf(np.random.standard_normal((B, D_H))),
           "n_prev": bf(np.random.uniform(size=(B, D_H)))}
    for g in ("i", "f", "z"):
        inp["W_" + g] = bf(np.random.standard_normal((D_IN, D_H)) * 0.5 / np.sqrt(D_IN) / s[:, None])
        inp["b_" + g] = bf(np.random.standard_normal(D_H) * 0.3)
        inp["U_" + g] = bf(np.random.standard_normal((D_H, D_H)) * 0.5 / np.sqrt(D_H) / t[:, None])
    return inp


def reference(x, h_prev, c_prev, n_prev, W_i, b_i, U_i, W_f, b_f, U_f, W_z, b_z, U_z):
    xq = mxq(f64(x), 1, "e4m3")
    hq = mxq(f64(h_prev), 1, "e4m3")
    i = np.exp((xq @ mxq(f64(W_i), 0, "e4m3")) + f64(b_i) + (hq @ mxq(f64(U_i), 0, "e4m3")))
    f = np.exp((xq @ mxq(f64(W_f), 0, "e4m3")) + f64(b_f) + (hq @ mxq(f64(U_f), 0, "e4m3")))
    z = np.tanh((xq @ mxq(f64(W_z), 0, "e4m3")) + f64(b_z) + (hq @ mxq(f64(U_z), 0, "e4m3")))
    c = f * f64(c_prev) + i * z
    n = f * f64(n_prev) + i
    return (c, n)

@@ -1,0 +1,287 @@
+from contextlib import ExitStack
+
+import concourse.mybir as mybir
+from concourse.masks import make_identity
+
+FLOPS = 6 * 2 * 512 * 1024 * 1024
+
+BF16 = mybir.dt.bfloat16
+F32 = mybir.dt.float32
+U32 = mybir.dt.uint32
+U8 = mybir.dt.uint8
+FP8X4 = mybir.dt.float8_e4m3fn_x4
+ACT = mybir.ActivationFunctionType
+ALU = mybir.AluOpType
+
+P = 128
+RAW_SLOTS = 6
+V_COLS_IF = 320
+V_COLS_Z = 0
+
+
+def tile_slstmcell_pa_kernel(
+    tc, x, h_prev, c_prev, n_prev, W_i, b_i, U_i, W_f, b_f, U_f, W_z, b_z, U_z, out_0, out_1
+):
+    nc = tc.nc
+    with ExitStack() as ctx:
+        const = ctx.enter_context(tc.tile_pool(name="const", bufs=1))
+        keep = ctx.enter_context(tc.tile_pool(name="keep", bufs=1))
+        rawp = ctx.enter_context(tc.tile_pool(name="rawp", bufs=RAW_SLOTS))
+        grpp = ctx.enter_context(tc.tile_pool(name="grpp", bufs=4))
+        gxp = ctx.enter_context(tc.tile_pool(name="gxp", bufs=2))
+        gatep = ctx.enter_context(tc.tile_pool(name="gatep", bufs=3))
+        tmpp = ctx.enter_context(tc.tile_pool(name="tmpp", bufs=2))
+        accp = ctx.enter_context(tc.psum_pool(name="accp", bufs=4))
+        trp = ctx.enter_context(tc.psum_pool(name="trp", bufs=4))
+
+        ident32 = const.tile([P, P], F32)
+        make_identity(nc, ident32[:])
+        ident16 = const.tile([P, P], BF16)
+        make_identity(nc, ident16[:])
+
+        bias_rows = const.tile([P, P], BF16)
+        nc.vector.memset(bias_rows[:], 0.0)
+        for g, b in enumerate((b_i, b_f, b_z)):
+            nc.scalar.dma_start(
+                out=bias_rows[8 * g : 8 * g + 8, :], in_=b.rearrange("(m c) -> m c", c=P)
+            )
+
+        codes = [keep.tile([P, 1024], U32, name="codes%d" % c, align_bytes=64) for c in range(12)]
+        planes = [keep.tile([P, 1024], U8, name="planes%d" % c, align_bytes=64) for c in range(12)]
+        xcodes = [keep.tile([P, 512], U32, name="xcodes%d" % c, align_bytes=64) for c in range(4)]
+        xplanes = [keep.tile([P, 512], U8, name="xplanes%d" % c, align_bytes=64) for c in range(4)]
+        c_sb = keep.tile([P, 4, 1024], BF16)
+        n_sb = keep.tile([P, 4, 1024], BF16)
+        i_sb = [keep.tile([P, 512], F32, name="i_sb%d" % m) for m in range(8)]
+        c_out = [keep.tile([P, 4, 256], F32, name="c_out%d" % j) for j in range(4)]
+        n_out = [keep.tile([P, 4, 256], F32, name="n_out%d" % j) for j in range(4)]
+        bias_sb = const.tile([P, 24], F32)
+
+        out_c = out_0.rearrange("(p a) h -> p a h", a=4)
+        out_n = out_1.rearrange("(p a) h -> p a h", a=4)
+
+        weights = ((W_i, U_i), (W_f, U_f), (W_z, U_z))
+        load_order = [("w", 0, 0), ("a", 0, 0), ("w", 0, 1), ("a", 1, 0), ("w", 0, 2), ("w", 0, 3)]
+        load_order += [("w", g, c) for g in (1, 2) for c in range(4)]
+        raw_tiles = {}
+        state = {"next": 0}
+
+        def issue_next_load():
+            k = state["next"]
+            if k >= len(load_order):
+                return
+            state["next"] = k + 1
+            kind, g, c = load_order[k]
+            raw = rawp.tile([P, 4, 1024], BF16, tag="raw", name="raw%d" % k)
+            raw_tiles[load_order[k]] = raw
+            if kind == "w":
+                w = weights[g][c // 2]
+                r0 = 512 * (c % 2)
+                nc.sync.dma_start(
+                    out=raw[:].rearrange("p (u e) n -> p u e n", u=2),
+                    in_=w[r0 : r0 + 512, :].rearrange("(u p e) n -> p u e n", u=2, e=2),
+                )
+            else:
+                src = x if g == 0 else h_prev
+                nc.sync.dma_start(out=raw[:], in_=src.rearrange("(p a) k -> p a k", a=4))
+            if load_order[k] == ("w", 1, 3):
+                nc.sync.dma_start(out=c_sb[:], in_=c_prev.rearrange("(p a) h -> p a h", a=4))
+                nc.sync.dma_start(out=n_sb[:], in_=n_prev.rearrange("(p a) h -> p a h", a=4))
+
+        for k in range(RAW_SLOTS):
+            issue_next_load()
+
+        bias_ps = trp.tile([P, P], BF16, tag="tr")
+        nc.tensor.transpose(bias_ps[:], bias_rows[:], ident16[:])
+        nc.vector.tensor_copy(out=bias_sb[:], in_=bias_ps[:, 0:24])
+
+        pending = []
+
+        def flush_quant(keep_last=0):
+            for q in range(len(pending) - keep_last):
+                grp, chunk, c0, ncols = pending.pop(0)
+                nc.vector.quantize_mx(
+                    out=codes[chunk][:, c0 : c0 + ncols].bitcast(FP8X4),
+                    scales=planes[chunk][:, c0 : c0 + ncols],
+                    in_=grp[:, 0:ncols, :].rearrange("p w t -> p (w t)"),
+                )
+
+        def unit(g, c, c0, ncols, vcols):
+            raw = raw_tiles[("w", g, c)]
+            grp = grpp.tile([P, 512, 4], BF16, tag="grp", name="grp_%d_%d_%d" % (g, c, c0), align_bytes=64)
+            if vcols > 0:
+                nc.vector.tensor_copy(
+                    out=grp[:, 0:vcols, :].rearrange("p (c i) t -> p c t i", i=4),
+                    in_=raw[:, :, c0 : c0 + vcols].rearrange("p t (c i) -> p c t i", i=4),
+                )
+            if vcols < ncols:
+                nc.scalar.copy(
+                    out=grp[:, vcols:ncols, :].rearrange("p (c i) t -> p c t i", i=4),
+                    in_=raw[:, :, c0 + vcols : c0 + ncols].rearrange("p t (c i) -> p c t i", i=4),
+                )
+            pending.append((grp, 4 * g + c, c0, ncols))
+            flush_quant(keep_last=1)
+
+        def activations(s):
+            raw = raw_tiles[("a", s, 0)]
+            words = raw[:].bitcast(F32)
+            for g in range(2):
+                gx = gxp.tile([P, 512, 4], BF16, tag="gx", name="gx_%d_%d" % (s, g), align_bytes=64)
+                gx32 = gx[:].bitcast(F32)
+                for half in range(2):
+                    bank = trp.tile([P, 2, 2, P], F32, tag="tr", name="xt_%d_%d_%d" % (s, g, half))
+                    for a in range(2):
+                        for u in range(2):
+                            w0 = 256 * g + 128 * u
+                            nc.tensor.transpose(
+                                bank[:, a, u, :], words[:, 2 * half + a, w0 : w0 + 128], ident32[:]
+                            )
+                    nc.scalar.copy(
+                        out=gx32[:, 256 * half : 256 * half + 256, :].rearrange(
+                            "p (a b) u -> p a b u", a=2
+                        ),
+                        in_=bank[:].rearrange("p a u b -> p a b u"),
+                    )
+                nc.vector.quantize_mx(
+                    out=xcodes[2 * s + g][:].bitcast(FP8X4),
+                    scales=xplanes[2 * s + g][:],
+                    in_=gx[:].rearrange("p w t -> p (w t)"),
+                )
+
+        accs = {}
+
+        def mx(g, tiles):
+            flush_quant()
+            for m in tiles:
+                accs[(g, m)] = accp.tile([P, 512], F32, tag="acc", name="acc_%d_%d" % (g, m))
+            for c in range(4):
+                for m in tiles:
+                    nc.tensor.matmul_mx(
+                        out=accs[(g, m)][:],
+                        lhsT=codes[4 * g + c][:, P * m : P * m + P].bitcast(FP8X4),
+                        lhsT_scale=planes[4 * g + c][:, P * m : P * m + P],
+                        rhs=xcodes[c][:].bitcast(FP8X4),
+                        rhs_scale=xplanes[c][:],
+                        start=(c == 0),
+                        stop=(c == 3),
+                    )
+
+        def gate_act(g, m, dst):
+            nc.scalar.activation(
+                out=dst,
+                in_=accs[(g, m)][:],
+                func=(ACT.Tanh if g == 2 else ACT.Exp),
+                bias=bias_sb[:, 8 * g + m : 8 * g + m + 1],
+                scale=1.0,
+            )
+
+        def flip(src, name):
+            bank = trp.tile([P, 4, P], F32, tag="tr", name=name)
+            for a in range(4):
+                nc.tensor.transpose(bank[:, a, :], src[:, P * a : P * a + P], ident32[:])
+            return bank
+
+        def act_i(m):
+            gate_act(0, m, i_sb[m][:])
+
+        def f_epilogue(m):
+            f_sb = gatep.tile([P, 512], F32, tag="f", name="f_sb%d" % m)
+            gate_act(1, m, f_sb[:])
+            fT = flip(f_sb, "fT%d" % m)
+            iT = flip(i_sb[m], "iT%d" % m)
+            j, off = m // 2, P * (m % 2)
+            cols = slice(P * m, P * m + P)
+            nc.vector.tensor_tensor(
+                out=c_out[j][:, :, off : off + P], in0=fT[:], in1=c_sb[:, :, cols], op=ALU.mult
+            )
+            fn = tmpp.tile([P, 4, P], F32, tag="fn", name="fn%d" % m)
+            nc.vector.tensor_tensor(out=fn[:], in0=fT[:], in1=n_sb[:, :, cols], op=ALU.mult)
+            nc.vector.tensor_tensor(
+                out=n_out[j][:, :, off : off + P], in0=iT[:], in1=fn[:], op=ALU.add
+            )
+            if m % 2 == 1:
+                nc.sync.dma_start(out=out_n[:, :, 256 * j : 256 * j + 256], in_=n_out[j][:])
+
+        def z_epilogue(m):
+            z_sb = gatep.tile([P, 512], F32, tag="z", name="z_sb%d" % m)
+            gate_act(2, m, z_sb[:])
+            iz = gatep.tile([P, 512], F32, tag="iz", name="iz%d" % m)
+            nc.vector.tensor_tensor(out=iz[:], in0=i_sb[m][:], in1=z_sb[:], op=ALU.mult)
+            izT = flip(iz, "izT%d" % m)
+            j, off = m // 2, P * (m % 2)
+            nc.vector.tensor_tensor(
+                out=c_out[j][:, :, off : off + P],
+                in0=izT[:],
+                in1=c_out[j][:, :, off : off + P],
+                op=ALU.add,
+            )
+            if m % 2 == 1:
+                nc.sync.dma_start(out=out_c[:, :, 256 * j : 256 * j + 256], in_=c_out[j][:])
+
+        def chunk_units(g, c, vcols):
+            unit(g, c, 0, 512, vcols)
+            unit(g, c, 512, 512, vcols)
+            issue_next_load()
+
+        chunk_units(0, 0, V_COLS_IF)
+        activations(0)
+        issue_next_load()
+        chunk_units(0, 1, V_COLS_IF)
+        activations(1)
+        issue_next_load()
+        chunk_units(0, 2, V_COLS_IF)
+        chunk_units(0, 3, V_COLS_IF)
+
+        chunk_units(1, 0, V_COLS_IF)
+        mx(0, (0, 1, 2, 3))
+        act_i(0)
+        act_i(1)
+        unit(1, 1, 0, 512, V_COLS_IF)
+        act_i(2)
+        act_i(3)
+        mx(0, (4, 5, 6, 7))
+        unit(1, 1, 512, 512, V_COLS_IF)
+        issue_next_load()
+        unit(1, 2, 0, 512, V_COLS_IF)
+        act_i(4)
+        act_i(5)
+        unit(1, 2, 512, 512, V_COLS_IF)
+        issue_next_load()
+        act_i(6)
+        act_i(7)
+        chunk_units(1, 3, V_COLS_IF)
+
+        mx(1, (0, 1, 2, 3))
+        unit(2, 0, 0, 512, V_COLS_Z)
+        f_epilogue(0)
+        f_epilogue(1)
+        unit(2, 1, 0, 512, V_COLS_Z)
+        f_epilogue(2)
+        f_epilogue(3)
+        mx(1, (4, 5, 6, 7))
+        unit(2, 2, 0, 512, V_COLS_Z)
+        f_epilogue(4)
+        f_epilogue(5)
+        unit(2, 3, 0, 512, V_COLS_Z)
+        f_epilogue(6)
+        f_epilogue(7)
+
+        mx(2, (0, 1, 2, 3))
+        unit(2, 0, 512, 256, 0)
+        unit(2, 1, 512, 256, 0)
+        z_epilogue(0)
+        z_epilogue(1)
+        unit(2, 2, 512, 256, 0)
+        unit(2, 3, 512, 256, 0)
+        z_epilogue(2)
+        z_epilogue(3)
+        mx(2, (4, 5))
+        unit(2, 0, 768, 256, 0)
+        unit(2, 1, 768, 256, 0)
+        z_epilogue(4)
+        unit(2, 2, 768, 256, 0)
+        z_epilogue(5)
+        unit(2, 3, 768, 256, 0)
+        mx(2, (6, 7))
+        z_epilogue(6)
+        z_epilogue(7)

@@ -15,8 +15,14 @@ ALU = mybir.AluOpType
 
 P = 128
 RAW_SLOTS = 6
-V_COLS_IF = 320
-V_COLS_Z = 0
+PINNED = False
+V_COLS_F = 288
+V_COLS_I = 224
+Z_V_CHUNKS = (2, 2, 2, 2, 2, 2, 2, 2)
+IZ_ON_G = (0, 1, 2, 3, 4, 5, 6)
+C_STORES = ((0, 1), (2, 3), (4, 5), (6,), (7,))
+N_STORES = ((0, 1), (2, 3), (4, 5), (6, 7))
+GF, GI, GZ = 0, 1, 2
 
 
 def tile_slstmcell_pa_kernel(
@@ -24,27 +30,28 @@ def tile_slstmcell_pa_kernel(
 ):
     nc = tc.nc
     with ExitStack() as ctx:
+        if PINNED:
+            ctx.enter_context(tc.manual_schedule())
         const = ctx.enter_context(tc.tile_pool(name="const", bufs=1))
         keep = ctx.enter_context(tc.tile_pool(name="keep", bufs=1))
         rawp = ctx.enter_context(tc.tile_pool(name="rawp", bufs=RAW_SLOTS))
         grpp = ctx.enter_context(tc.tile_pool(name="grpp", bufs=4))
         gxp = ctx.enter_context(tc.tile_pool(name="gxp", bufs=2))
         gatep = ctx.enter_context(tc.tile_pool(name="gatep", bufs=3))
-        tmpp = ctx.enter_context(tc.tile_pool(name="tmpp", bufs=2))
         accp = ctx.enter_context(tc.psum_pool(name="accp", bufs=4))
-        trp = ctx.enter_context(tc.psum_pool(name="trp", bufs=4))
+        trp = ctx.enter_context(tc.psum_pool(name="trp", bufs=2))
+        flexp = ctx.enter_context(tc.psum_pool(name="flexp", bufs=2))
 
+        weights = ((W_f, U_f), (W_i, U_i), (W_z, U_z))
+        biases = (b_f, b_i, b_z)
+
+        bias_rows = const.tile([P, P], BF16)
+        nc.vector.memset(bias_rows[:], 0.0)
         ident32 = const.tile([P, P], F32)
         make_identity(nc, ident32[:])
         ident16 = const.tile([P, P], BF16)
         make_identity(nc, ident16[:])
-
-        bias_rows = const.tile([P, P], BF16)
-        nc.vector.memset(bias_rows[:], 0.0)
-        for g, b in enumerate((b_i, b_f, b_z)):
-            nc.scalar.dma_start(
-                out=bias_rows[8 * g : 8 * g + 8, :], in_=b.rearrange("(m c) -> m c", c=P)
-            )
+        bias_sb = const.tile([P, 24], F32)
 
         codes = [keep.tile([P, 1024], U32, name="codes%d" % c, align_bytes=64) for c in range(12)]
         planes = [keep.tile([P, 1024], U8, name="planes%d" % c, align_bytes=64) for c in range(12)]
@@ -53,25 +60,41 @@ def tile_slstmcell_pa_kernel(
         c_sb = keep.tile([P, 4, 1024], BF16)
         n_sb = keep.tile([P, 4, 1024], BF16)
         i_sb = [keep.tile([P, 512], F32, name="i_sb%d" % m) for m in range(8)]
-        c_out = [keep.tile([P, 4, 256], F32, name="c_out%d" % j) for j in range(4)]
-        n_out = [keep.tile([P, 4, 256], F32, name="n_out%d" % j) for j in range(4)]
-        bias_sb = const.tile([P, 24], F32)
+        c_out = [keep.tile([P, 4, P * len(grp)], F32, name="c_out%d" % grp[0]) for grp in C_STORES]
+        n_out = [keep.tile([P, 4, P * len(grp)], F32, name="n_out%d" % grp[0]) for grp in N_STORES]
 
         out_c = out_0.rearrange("(p a) h -> p a h", a=4)
         out_n = out_1.rearrange("(p a) h -> p a h", a=4)
 
-        weights = ((W_i, U_i), (W_f, U_f), (W_z, U_z))
         load_order = [("w", 0, 0), ("a", 0, 0), ("w", 0, 1), ("a", 1, 0), ("w", 0, 2), ("w", 0, 3)]
-        load_order += [("w", g, c) for g in (1, 2) for c in range(4)]
+        load_order += [("w", 1, 0), ("c", 0, 0), ("c", 1, 0), ("w", 1, 1), ("w", 1, 2), ("w", 1, 3)]
+        load_order += [("w", 2, c) for c in range(4)]
         raw_tiles = {}
-        state = {"next": 0}
+        state = {"load": 0}
 
         def issue_next_load():
-            k = state["next"]
+            k = state["load"]
             if k >= len(load_order):
                 return
-            state["next"] = k + 1
+            state["load"] = k + 1
             kind, g, c = load_order[k]
+            if kind == "c":
+                dst, src = ((c_sb, c_prev), (n_sb, n_prev))[g]
+                nc.sync.dma_start(out=dst[:], in_=src.rearrange("(p a) h -> p a h", a=4))
+                issue_next_load()
+                return
+            if k == 0:
+                halves = rawp.tile([P, 2, 4, 512], BF16, tag="raw")
+                raw_tiles["first"] = halves
+                for b in range(2):
+                    for u in range(2):
+                        nc.sync.dma_start(
+                            out=halves[:, b, 2 * u : 2 * u + 2, :],
+                            in_=weights[0][0][256 * u : 256 * u + 256, 512 * b : 512 * b + 512].rearrange(
+                                "(p e) n -> p e n", e=2
+                            ),
+                        )
+                return
             raw = rawp.tile([P, 4, 1024], BF16, tag="raw", name="raw%d" % k)
             raw_tiles[load_order[k]] = raw
             if kind == "w":
@@ -84,204 +107,266 @@ def tile_slstmcell_pa_kernel(
             else:
                 src = x if g == 0 else h_prev
                 nc.sync.dma_start(out=raw[:], in_=src.rearrange("(p a) k -> p a k", a=4))
-            if load_order[k] == ("w", 1, 3):
-                nc.sync.dma_start(out=c_sb[:], in_=c_prev.rearrange("(p a) h -> p a h", a=4))
-                nc.sync.dma_start(out=n_sb[:], in_=n_prev.rearrange("(p a) h -> p a h", a=4))
 
         for k in range(RAW_SLOTS):
             issue_next_load()
-
-        bias_ps = trp.tile([P, P], BF16, tag="tr")
-        nc.tensor.transpose(bias_ps[:], bias_rows[:], ident16[:])
-        nc.vector.tensor_copy(out=bias_sb[:], in_=bias_ps[:, 0:24])
-
-        pending = []
-
-        def flush_quant(keep_last=0):
-            for q in range(len(pending) - keep_last):
-                grp, chunk, c0, ncols = pending.pop(0)
-                nc.vector.quantize_mx(
-                    out=codes[chunk][:, c0 : c0 + ncols].bitcast(FP8X4),
-                    scales=planes[chunk][:, c0 : c0 + ncols],
-                    in_=grp[:, 0:ncols, :].rearrange("p w t -> p (w t)"),
-                )
-
-        def unit(g, c, c0, ncols, vcols):
-            raw = raw_tiles[("w", g, c)]
-            grp = grpp.tile([P, 512, 4], BF16, tag="grp", name="grp_%d_%d_%d" % (g, c, c0), align_bytes=64)
-            if vcols > 0:
-                nc.vector.tensor_copy(
-                    out=grp[:, 0:vcols, :].rearrange("p (c i) t -> p c t i", i=4),
-                    in_=raw[:, :, c0 : c0 + vcols].rearrange("p t (c i) -> p c t i", i=4),
-                )
-            if vcols < ncols:
-                nc.scalar.copy(
-                    out=grp[:, vcols:ncols, :].rearrange("p (c i) t -> p c t i", i=4),
-                    in_=raw[:, :, c0 + vcols : c0 + ncols].rearrange("p t (c i) -> p c t i", i=4),
-                )
-            pending.append((grp, 4 * g + c, c0, ncols))
-            flush_quant(keep_last=1)
-
-        def activations(s):
-            raw = raw_tiles[("a", s, 0)]
-            words = raw[:].bitcast(F32)
-            for g in range(2):
-                gx = gxp.tile([P, 512, 4], BF16, tag="gx", name="gx_%d_%d" % (s, g), align_bytes=64)
-                gx32 = gx[:].bitcast(F32)
-                for half in range(2):
-                    bank = trp.tile([P, 2, 2, P], F32, tag="tr", name="xt_%d_%d_%d" % (s, g, half))
-                    for a in range(2):
-                        for u in range(2):
-                            w0 = 256 * g + 128 * u
-                            nc.tensor.transpose(
-                                bank[:, a, u, :], words[:, 2 * half + a, w0 : w0 + 128], ident32[:]
-                            )
-                    nc.scalar.copy(
-                        out=gx32[:, 256 * half : 256 * half + 256, :].rearrange(
-                            "p (a b) u -> p a b u", a=2
-                        ),
-                        in_=bank[:].rearrange("p a u b -> p a b u"),
+            if k == 1:
+                for g in range(3):
+                    nc.sync.dma_start(
+                        out=bias_rows[8 * g : 8 * g + 8, :],
+                        in_=biases[g].rearrange("(m c) -> m c", c=P),
                     )
-                nc.vector.quantize_mx(
-                    out=xcodes[2 * s + g][:].bitcast(FP8X4),
-                    scales=xplanes[2 * s + g][:],
-                    in_=gx[:].rearrange("p w t -> p (w t)"),
+
+        def regroup(eng, dst, src):
+            o = dst.rearrange("p (c i) t -> p c t i", i=4)
+            s = src.rearrange("p t (c i) -> p c t i", i=4)
+            if eng == "v":
+                nc.vector.tensor_copy(out=o, in_=s)
+            else:
+                nc.scalar.copy(out=o, in_=s)
+
+        grps = {}
+
+        def rg_unit(g, u, vcols):
+            c, c0 = u // 2, 512 * (u % 2)
+            if g == 0 and c == 0:
+                src = raw_tiles["first"][:, u]
+            else:
+                src = raw_tiles[("w", g, c)][:, :, c0 : c0 + 512]
+            grp = grpp.tile([P, 512, 4], BF16, tag="grp", name="grp_%d_%d" % (g, u), align_bytes=64)
+            grps[(g, u)] = grp
+            regroup("v", grp[:, 0:vcols, :], src[:, :, 0:vcols])
+            regroup("s", grp[:, vcols:512, :], src[:, :, vcols:512])
+
+        def q_unit(g, u):
+            c, c0 = u // 2, 512 * (u % 2)
+            nc.vector.quantize_mx(
+                out=codes[4 * g + c][:, c0 : c0 + 512].bitcast(FP8X4),
+                scales=planes[4 * g + c][:, c0 : c0 + 512],
+                in_=grps[(g, u)][:].rearrange("p w t -> p (w t)"),
+            )
+
+        def rg_ztile(m, v_chunks):
+            grp = grpp.tile([P, 512, 4], BF16, tag="grp", name="grp_z_%d" % m, align_bytes=64)
+            grps[(GZ, m)] = grp
+            for c in range(4):
+                raw = raw_tiles[("w", GZ, c)]
+                regroup(
+                    "v" if c >= 4 - v_chunks else "s",
+                    grp[:, P * c : P * c + P, :],
+                    raw[:, :, P * m : P * m + P],
                 )
+
+        def q_ztile(m):
+            c0 = 512 * (m % 2)
+            nc.vector.quantize_mx(
+                out=codes[8 + m // 2][:, c0 : c0 + 512].bitcast(FP8X4),
+                scales=planes[8 + m // 2][:, c0 : c0 + 512],
+                in_=grps[(GZ, m)][:].rearrange("p w t -> p (w t)"),
+            )
+
+        def stationary(g, m, c):
+            if g == GZ:
+                t, c0 = 8 + m // 2, 512 * (m % 2) + P * c
+            else:
+                t, c0 = 4 * g + c, P * m
+            return codes[t][:, c0 : c0 + P].bitcast(FP8X4), planes[t][:, c0 : c0 + P]
+
+        gxs = {}
+        banks = {}
+
+        def xt(s, g, half):
+            words = raw_tiles[("a", s, 0)][:].bitcast(F32)
+            bank = (trp, flexp)[half].tile([P, 2, 2, P], F32, tag="bank", name="xt_%d_%d_%d" % (s, g, half))
+            banks[(s, g, half)] = bank
+            for a in range(2):
+                for u in range(2):
+                    w0 = 256 * g + 128 * u
+                    nc.tensor.transpose(
+                        bank[:, a, u, :], words[:, 2 * half + a, w0 : w0 + 128], ident32[:]
+                    )
+
+        def xc(s, g, half):
+            if half == 0:
+                gxs[(s, g)] = gxp.tile([P, 512, 4], BF16, tag="gx", name="gx_%d_%d" % (s, g), align_bytes=64)
+            gx32 = gxs[(s, g)][:].bitcast(F32)
+            nc.scalar.copy(
+                out=gx32[:, 256 * half : 256 * half + 256, :].rearrange("p (a b) u -> p a b u", a=2),
+                in_=banks[(s, g, half)][:].rearrange("p a u b -> p a b u"),
+            )
+
+        def xq(s, g):
+            nc.vector.quantize_mx(
+                out=xcodes[2 * s + g][:].bitcast(FP8X4),
+                scales=xplanes[2 * s + g][:],
+                in_=gxs[(s, g)][:].rearrange("p w t -> p (w t)"),
+            )
 
         accs = {}
 
-        def mx(g, tiles):
-            flush_quant()
-            for m in tiles:
-                accs[(g, m)] = accp.tile([P, 512], F32, tag="acc", name="acc_%d_%d" % (g, m))
-            for c in range(4):
-                for m in tiles:
-                    nc.tensor.matmul_mx(
-                        out=accs[(g, m)][:],
-                        lhsT=codes[4 * g + c][:, P * m : P * m + P].bitcast(FP8X4),
-                        lhsT_scale=planes[4 * g + c][:, P * m : P * m + P],
-                        rhs=xcodes[c][:].bitcast(FP8X4),
-                        rhs_scale=xplanes[c][:],
-                        start=(c == 0),
-                        stop=(c == 3),
-                    )
+        def mx_pass(g, m, c, pool=None):
+            if c == 0:
+                pl = pool or accp
+                accs[(g, m)] = pl.tile([P, 512], F32, tag="bank", name="acc_%d_%d" % (g, m))
+            lhsT, lhsT_scale = stationary(g, m, c)
+            nc.tensor.matmul_mx(
+                out=accs[(g, m)][:],
+                lhsT=lhsT,
+                lhsT_scale=lhsT_scale,
+                rhs=xcodes[c][:].bitcast(FP8X4),
+                rhs_scale=xplanes[c][:],
+                start=(c == 0),
+                stop=(c == 3),
+            )
 
-        def gate_act(g, m, dst):
+        def mx(g, m, pool=None):
+            for c in range(4):
+                mx_pass(g, m, c, pool)
+
+        sb = {}
+
+        def gate_act(g, m):
+            if g == GI:
+                dst = i_sb[m]
+            else:
+                dst = gatep.tile([P, 512], F32, tag="g%d" % g, name="gate_%d_%d" % (g, m))
+            sb[(g, m)] = dst
             nc.scalar.activation(
-                out=dst,
+                out=dst[:],
                 in_=accs[(g, m)][:],
-                func=(ACT.Tanh if g == 2 else ACT.Exp),
+                func=(ACT.Tanh if g == GZ else ACT.Exp),
                 bias=bias_sb[:, 8 * g + m : 8 * g + m + 1],
                 scale=1.0,
             )
 
-        def flip(src, name):
-            bank = trp.tile([P, 4, P], F32, tag="tr", name=name)
+        flipped = {}
+
+        def flip(key, pool=None):
+            bank = (pool or trp).tile([P, 4, P], F32, tag="bank", name="T_%s_%d" % key)
+            flipped[key] = bank
+            src = sb[key]
             for a in range(4):
                 nc.tensor.transpose(bank[:, a, :], src[:, P * a : P * a + P], ident32[:])
-            return bank
 
-        def act_i(m):
-            gate_act(0, m, i_sb[m][:])
+        def part(tiles, groups, m):
+            for j, grp in enumerate(groups):
+                if m in grp:
+                    off = P * grp.index(m)
+                    return tiles[j][:, :, off : off + P]
 
-        def f_epilogue(m):
-            f_sb = gatep.tile([P, 512], F32, tag="f", name="f_sb%d" % m)
-            gate_act(1, m, f_sb[:])
-            fT = flip(f_sb, "fT%d" % m)
-            iT = flip(i_sb[m], "iT%d" % m)
-            j, off = m // 2, P * (m % 2)
+        def store_if_full(dram, tiles, groups, m):
+            for j, grp in enumerate(groups):
+                if m == grp[-1]:
+                    nc.sync.dma_start(out=dram[:, :, P * grp[0] : P * grp[-1] + P], in_=tiles[j][:])
+
+        def v_fc_fn(m):
             cols = slice(P * m, P * m + P)
-            nc.vector.tensor_tensor(
-                out=c_out[j][:, :, off : off + P], in0=fT[:], in1=c_sb[:, :, cols], op=ALU.mult
-            )
-            fn = tmpp.tile([P, 4, P], F32, tag="fn", name="fn%d" % m)
-            nc.vector.tensor_tensor(out=fn[:], in0=fT[:], in1=n_sb[:, :, cols], op=ALU.mult)
-            nc.vector.tensor_tensor(
-                out=n_out[j][:, :, off : off + P], in0=iT[:], in1=fn[:], op=ALU.add
-            )
-            if m % 2 == 1:
-                nc.sync.dma_start(out=out_n[:, :, 256 * j : 256 * j + 256], in_=n_out[j][:])
+            fT = flipped[(GF, m)]
+            nc.vector.tensor_tensor(out=part(c_out, C_STORES, m), in0=fT[:], in1=c_sb[:, :, cols], op=ALU.mult)
+            nc.vector.tensor_tensor(out=part(n_out, N_STORES, m), in0=fT[:], in1=n_sb[:, :, cols], op=ALU.mult)
 
-        def z_epilogue(m):
-            z_sb = gatep.tile([P, 512], F32, tag="z", name="z_sb%d" % m)
-            gate_act(2, m, z_sb[:])
+        def v_n(m):
+            nc.vector.tensor_tensor(
+                out=part(n_out, N_STORES, m), in0=flipped[(GI, m)][:], in1=part(n_out, N_STORES, m), op=ALU.add
+            )
+            store_if_full(out_n, n_out, N_STORES, m)
+
+        def v_iz(m):
             iz = gatep.tile([P, 512], F32, tag="iz", name="iz%d" % m)
-            nc.vector.tensor_tensor(out=iz[:], in0=i_sb[m][:], in1=z_sb[:], op=ALU.mult)
-            izT = flip(iz, "izT%d" % m)
-            j, off = m // 2, P * (m % 2)
+            sb[("iz", m)] = iz
+            eng = nc.gpsimd if m in IZ_ON_G else nc.vector
+            eng.tensor_tensor(out=iz[:], in0=i_sb[m][:], in1=sb[(GZ, m)][:], op=ALU.mult)
+
+        def v_c(m):
             nc.vector.tensor_tensor(
-                out=c_out[j][:, :, off : off + P],
-                in0=izT[:],
-                in1=c_out[j][:, :, off : off + P],
-                op=ALU.add,
+                out=part(c_out, C_STORES, m), in0=flipped[("iz", m)][:], in1=part(c_out, C_STORES, m), op=ALU.add
             )
-            if m % 2 == 1:
-                nc.sync.dma_start(out=out_c[:, :, 256 * j : 256 * j + 256], in_=c_out[j][:])
+            store_if_full(out_c, c_out, C_STORES, m)
 
-        def chunk_units(g, c, vcols):
-            unit(g, c, 0, 512, vcols)
-            unit(g, c, 512, 512, vcols)
-            issue_next_load()
+        def first_half_passes(g, c):
+            for m in range(4):
+                mx_pass(g, m, c)
 
-        chunk_units(0, 0, V_COLS_IF)
-        activations(0)
+        rg_unit(GF, 0, V_COLS_F)
+        rg_unit(GF, 1, V_COLS_F)
         issue_next_load()
-        chunk_units(0, 1, V_COLS_IF)
-        activations(1)
+        q_unit(GF, 0)
+        for g in range(2):
+            for half in range(2):
+                xt(0, g, half)
+                xc(0, g, half)
         issue_next_load()
-        chunk_units(0, 2, V_COLS_IF)
-        chunk_units(0, 3, V_COLS_IF)
-
-        chunk_units(1, 0, V_COLS_IF)
-        mx(0, (0, 1, 2, 3))
-        act_i(0)
-        act_i(1)
-        unit(1, 1, 0, 512, V_COLS_IF)
-        act_i(2)
-        act_i(3)
-        mx(0, (4, 5, 6, 7))
-        unit(1, 1, 512, 512, V_COLS_IF)
+        q_unit(GF, 1)
+        xq(0, 0)
+        rg_unit(GF, 2, V_COLS_F)
+        xq(0, 1)
+        first_half_passes(GF, 0)
+        bias_ps = trp.tile([P, P], BF16, tag="bank")
+        nc.tensor.transpose(bias_ps[:], bias_rows[:], ident16[:])
+        nc.vector.tensor_copy(out=bias_sb[:], in_=bias_ps[:, 0:24])
+        rg_unit(GF, 3, V_COLS_F)
         issue_next_load()
-        unit(1, 2, 0, 512, V_COLS_IF)
-        act_i(4)
-        act_i(5)
-        unit(1, 2, 512, 512, V_COLS_IF)
+        q_unit(GF, 2)
+        for g in range(2):
+            for half in range(2):
+                xt(1, g, half)
+                xc(1, g, half)
         issue_next_load()
-        act_i(6)
-        act_i(7)
-        chunk_units(1, 3, V_COLS_IF)
+        first_half_passes(GF, 1)
+        q_unit(GF, 3)
+        xq(1, 0)
+        rg_unit(GF, 4, V_COLS_F)
+        xq(1, 1)
+        rg_unit(GF, 5, V_COLS_F)
+        issue_next_load()
+        q_unit(GF, 4)
+        first_half_passes(GF, 2)
+        rg_unit(GF, 6, V_COLS_F)
+        q_unit(GF, 5)
+        rg_unit(GF, 7, V_COLS_F)
+        issue_next_load()
+        q_unit(GF, 6)
+        first_half_passes(GF, 3)
 
-        mx(1, (0, 1, 2, 3))
-        unit(2, 0, 0, 512, V_COLS_Z)
-        f_epilogue(0)
-        f_epilogue(1)
-        unit(2, 1, 0, 512, V_COLS_Z)
-        f_epilogue(2)
-        f_epilogue(3)
-        mx(1, (4, 5, 6, 7))
-        unit(2, 2, 0, 512, V_COLS_Z)
-        f_epilogue(4)
-        f_epilogue(5)
-        unit(2, 3, 0, 512, V_COLS_Z)
-        f_epilogue(6)
-        f_epilogue(7)
+        for s in range(8):
+            rg_unit(GI, s, V_COLS_I)
+            if s % 2 == 1:
+                issue_next_load()
+            gate_act(GF, s)
+            if s == 0:
+                q_unit(GF, 7)
+            else:
+                q_unit(GI, s - 1)
+            flip((GF, s))
+            if s < 4:
+                mx(GF, s + 4, flexp)
+            if s % 2 == 1:
+                first_half_passes(GI, s // 2)
+            if s > 0:
+                v_fc_fn(s - 1)
 
-        mx(2, (0, 1, 2, 3))
-        unit(2, 0, 512, 256, 0)
-        unit(2, 1, 512, 256, 0)
-        z_epilogue(0)
-        z_epilogue(1)
-        unit(2, 2, 512, 256, 0)
-        unit(2, 3, 512, 256, 0)
-        z_epilogue(2)
-        z_epilogue(3)
-        mx(2, (4, 5))
-        unit(2, 0, 768, 256, 0)
-        unit(2, 1, 768, 256, 0)
-        z_epilogue(4)
-        unit(2, 2, 768, 256, 0)
-        z_epilogue(5)
-        unit(2, 3, 768, 256, 0)
-        mx(2, (6, 7))
-        z_epilogue(6)
-        z_epilogue(7)
+        rg_ztile(0, Z_V_CHUNKS[0])
+        q_unit(GI, 7)
+        q_ztile(0)
+        rg_ztile(1, Z_V_CHUNKS[1])
+        v_fc_fn(7)
+        mx(GZ, 0, flexp)
+        gate_act(GI, 0)
+        flip((GI, 0))
+        for s in range(8):
+            if s < 7:
+                q_ztile(s + 1)
+                mx(GZ, s + 1, flexp)
+            if s < 6:
+                rg_ztile(s + 2, Z_V_CHUNKS[s + 2])
+            gate_act(GZ, s)
+            if s < 7:
+                gate_act(GI, s + 1)
+            v_iz(s)
+            flip(("iz", s))
+            if s < 7:
+                flip((GI, s + 1))
+            if 4 <= s + 3 < 8:
+                mx(GI, s + 3)
+            v_n(s)
+            v_c(s)

@@ -19,7 +19,7 @@ PINNED = False
 V_COLS_F = 288
 V_COLS_I = 224
 Z_V_CHUNKS = (2, 2, 2, 2, 2, 2, 2, 2)
-IZ_ON_G = (0, 1, 2, 3, 4, 5, 6)
+IZ_ON_G = ()
 C_STORES = ((0, 1), (2, 3), (4, 5), (6,), (7,))
 N_STORES = ((0, 1), (2, 3), (4, 5), (6, 7))
 GF, GI, GZ = 0, 1, 2

@@ -17,8 +17,8 @@ P = 128
 RAW_SLOTS = 6
 PINNED = False
 V_COLS_F = 288
-V_COLS_I = 224
-Z_V_CHUNKS = (2, 2, 2, 2, 2, 2, 2, 2)
+V_COLS_I = 160
+Z_V_CHUNKS = (1, 1, 1, 1, 1, 1, 1, 1)
 IZ_ON_G = ()
 C_STORES = ((0, 1), (2, 3), (4, 5), (6,), (7,))
 N_STORES = ((0, 1), (2, 3), (4, 5), (6, 7))

@@ -17,11 +17,9 @@ P = 128
 RAW_SLOTS = 6
 PINNED = False
 V_COLS_F = 288
-V_COLS_I = 160
-Z_V_CHUNKS = (1, 1, 1, 1, 1, 1, 1, 1)
-IZ_ON_G = ()
-C_STORES = ((0, 1), (2, 3), (4, 5), (6,), (7,))
-N_STORES = ((0, 1), (2, 3), (4, 5), (6, 7))
+V_COLS_I = 192
+Z_V_CHUNKS = (1, 2, 1, 2, 1, 2, 1, 2)
+STORES = ((0, 1), (2, 3), (4, 5), (6,), (7,))
 GF, GI, GZ = 0, 1, 2
 
 
@@ -57,11 +55,9 @@ def tile_slstmcell_pa_kernel(
         planes = [keep.tile([P, 1024], U8, name="planes%d" % c, align_bytes=64) for c in range(12)]
         xcodes = [keep.tile([P, 512], U32, name="xcodes%d" % c, align_bytes=64) for c in range(4)]
         xplanes = [keep.tile([P, 512], U8, name="xplanes%d" % c, align_bytes=64) for c in range(4)]
-        c_sb = keep.tile([P, 4, 1024], BF16)
-        n_sb = keep.tile([P, 4, 1024], BF16)
+        cn_sb = keep.tile([P, 2, 4, 1024], BF16)
         i_sb = [keep.tile([P, 512], F32, name="i_sb%d" % m) for m in range(8)]
-        c_out = [keep.tile([P, 4, P * len(grp)], F32, name="c_out%d" % grp[0]) for grp in C_STORES]
-        n_out = [keep.tile([P, 4, P * len(grp)], F32, name="n_out%d" % grp[0]) for grp in N_STORES]
+        cn_out = [keep.tile([P, 2, 4, P * len(grp)], F32, name="cn_out%d" % grp[0]) for grp in STORES]
 
         out_c = out_0.rearrange("(p a) h -> p a h", a=4)
         out_n = out_1.rearrange("(p a) h -> p a h", a=4)
@@ -79,8 +75,8 @@ def tile_slstmcell_pa_kernel(
             state["load"] = k + 1
             kind, g, c = load_order[k]
             if kind == "c":
-                dst, src = ((c_sb, c_prev), (n_sb, n_prev))[g]
-                nc.sync.dma_start(out=dst[:], in_=src.rearrange("(p a) h -> p a h", a=4))
+                src = (c_prev, n_prev)[g]
+                nc.sync.dma_start(out=cn_sb[:, g], in_=src.rearrange("(p a) h -> p a h", a=4))
                 issue_next_load()
                 return
             if k == 0:
@@ -248,40 +244,43 @@ def tile_slstmcell_pa_kernel(
             for a in range(4):
                 nc.tensor.transpose(bank[:, a, :], src[:, P * a : P * a + P], ident32[:])
 
-        def part(tiles, groups, m):
-            for j, grp in enumerate(groups):
+        def part(m):
+            for j, grp in enumerate(STORES):
                 if m in grp:
                     off = P * grp.index(m)
-                    return tiles[j][:, :, off : off + P]
+                    return cn_out[j][:, :, :, off : off + P]
 
-        def store_if_full(dram, tiles, groups, m):
-            for j, grp in enumerate(groups):
+        def store_if_full(which, m):
+            for j, grp in enumerate(STORES):
                 if m == grp[-1]:
-                    nc.sync.dma_start(out=dram[:, :, P * grp[0] : P * grp[-1] + P], in_=tiles[j][:])
+                    dram = (out_c, out_n)[which]
+                    nc.sync.dma_start(out=dram[:, :, P * grp[0] : P * grp[-1] + P], in_=cn_out[j][:, which])
 
         def v_fc_fn(m):
-            cols = slice(P * m, P * m + P)
             fT = flipped[(GF, m)]
-            nc.vector.tensor_tensor(out=part(c_out, C_STORES, m), in0=fT[:], in1=c_sb[:, :, cols], op=ALU.mult)
-            nc.vector.tensor_tensor(out=part(n_out, N_STORES, m), in0=fT[:], in1=n_sb[:, :, cols], op=ALU.mult)
+            nc.vector.tensor_tensor(
+                out=part(m),
+                in0=fT[:].unsqueeze(1).to_broadcast([P, 2, 4, P]),
+                in1=cn_sb[:, :, :, P * m : P * m + P],
+                op=ALU.mult,
+            )
 
         def v_n(m):
             nc.vector.tensor_tensor(
-                out=part(n_out, N_STORES, m), in0=flipped[(GI, m)][:], in1=part(n_out, N_STORES, m), op=ALU.add
+                out=part(m)[:, 1], in0=flipped[(GI, m)][:], in1=part(m)[:, 1], op=ALU.add
             )
-            store_if_full(out_n, n_out, N_STORES, m)
+            store_if_full(1, m)
 
         def v_iz(m):
             iz = gatep.tile([P, 512], F32, tag="iz", name="iz%d" % m)
             sb[("iz", m)] = iz
-            eng = nc.gpsimd if m in IZ_ON_G else nc.vector
-            eng.tensor_tensor(out=iz[:], in0=i_sb[m][:], in1=sb[(GZ, m)][:], op=ALU.mult)
+            nc.vector.tensor_tensor(out=iz[:], in0=i_sb[m][:], in1=sb[(GZ, m)][:], op=ALU.mult)
 
         def v_c(m):
             nc.vector.tensor_tensor(
-                out=part(c_out, C_STORES, m), in0=flipped[("iz", m)][:], in1=part(c_out, C_STORES, m), op=ALU.add
+                out=part(m)[:, 0], in0=flipped[("iz", m)][:], in1=part(m)[:, 0], op=ALU.add
             )
-            store_if_full(out_c, c_out, C_STORES, m)
+            store_if_full(0, m)
 
         def first_half_passes(g, c):
             for m in range(4):

@@ -15,7 +15,25 @@ ALU = mybir.AluOpType
 
 P = 128
 RAW_SLOTS = 6
-PINNED = False
+PINNED = True
+ORDER = (0, 1, 2, 3, 4, 5, 6, 7, 8, 9, 10, 13, 14, 11, 12, 15, 16, 18, 42, 17, 39, 19, 40, 20,
+    21, 22, 24, 25, 26, 27, 29, 23, 30, 31, 32, 34, 35, 36, 37, 28, 51, 41, 33, 52, 43, 38, 44, 45,
+    47, 46, 48, 49, 53, 54, 50, 57, 56, 58, 59, 60, 62, 63, 64, 65, 55, 67, 61, 82, 68, 69, 70, 72,
+    73, 74, 75, 66, 78, 77, 79, 71, 80, 83, 81, 76, 114, 84, 115, 85, 127, 86, 128, 87, 88, 90, 96, 89,
+    95, 91, 97, 92, 99, 93, 98, 94, 116, 107, 101, 129, 100, 106, 102, 109, 119, 103, 104, 118, 105, 122, 117, 130,
+    108, 120, 139, 121, 131, 110, 111, 138, 112, 113, 123, 124, 125, 126, 132, 135, 152, 133, 169, 134, 148, 137, 144, 145,
+    146, 147, 136, 140, 150, 141, 149, 142, 143, 154, 155, 156, 157, 153, 166, 168, 151, 162, 163, 164, 167, 165, 177, 171,
+    170, 172, 173, 174, 175, 178, 176, 190, 180, 181, 179, 182, 183, 158, 188, 159, 160, 191, 161, 184, 199, 185, 189, 186,
+    187, 192, 193, 194, 195, 197, 196, 200, 211, 198, 202, 212, 203, 204, 205, 201, 213, 210, 217, 206, 207, 218, 208, 215,
+    209, 226, 214, 216, 236, 273, 274, 219, 237, 275, 220, 222, 238, 221, 223, 224, 241, 225, 276, 231, 258, 301, 302, 239,
+    240, 303, 253, 232, 259, 233, 260, 234, 242, 263, 235, 254, 255, 286, 261, 256, 281, 257, 262, 304, 289, 327, 287, 328,
+    314, 282, 264, 283, 288, 284, 315, 285, 290, 343, 329, 330, 307, 291, 227, 228, 229, 230, 292, 243, 244, 312, 245, 246,
+    355, 251, 313, 308, 309, 310, 316, 252, 311, 356, 317, 335, 357, 358, 318, 340, 247, 248, 249, 250, 265, 266, 341, 267,
+    368, 268, 336, 277, 342, 337, 338, 279, 339, 344, 278, 269, 270, 271, 272, 345, 361, 293, 280, 294, 295, 296, 305, 366,
+    362, 367, 306, 363, 364, 370, 365, 346, 297, 298, 371, 299, 300, 369, 319, 320, 321, 322, 372, 390, 331, 391, 333, 323,
+    332, 324, 325, 326, 385, 347, 334, 348, 349, 350, 359, 386, 360, 387, 388, 389, 392, 351, 352, 353, 354, 405, 373, 374,
+    375, 376, 381, 383, 377, 382, 378, 379, 380, 406, 393, 384, 394, 395, 396, 401, 403, 397, 402, 398, 399, 400, 411, 407,
+    404, 408, 409, 410, 413, 412, 414)
 V_COLS_F = 288
 V_COLS_I = 192
 Z_V_CHUNKS = (1, 2, 1, 2, 1, 2, 1, 2)
@@ -40,11 +58,16 @@ def tile_slstmcell_pa_kernel(
         trp = ctx.enter_context(tc.psum_pool(name="trp", bufs=2))
         flexp = ctx.enter_context(tc.psum_pool(name="flexp", bufs=2))
 
+        ops = []
+
+        def later(fn, **kw):
+            ops.append((fn, kw))
+
         weights = ((W_f, U_f), (W_i, U_i), (W_z, U_z))
         biases = (b_f, b_i, b_z)
 
         bias_rows = const.tile([P, P], BF16)
-        nc.vector.memset(bias_rows[:], 0.0)
+        later(nc.vector.memset, ap=bias_rows[:], constant=0.0)
         ident32 = const.tile([P, P], F32)
         make_identity(nc, ident32[:])
         ident16 = const.tile([P, P], BF16)
@@ -76,7 +99,7 @@ def tile_slstmcell_pa_kernel(
             kind, g, c = load_order[k]
             if kind == "c":
                 src = (c_prev, n_prev)[g]
-                nc.sync.dma_start(out=cn_sb[:, g], in_=src.rearrange("(p a) h -> p a h", a=4))
+                later(nc.sync.dma_start, out=cn_sb[:, g], in_=src.rearrange("(p a) h -> p a h", a=4))
                 issue_next_load()
                 return
             if k == 0:
@@ -84,8 +107,7 @@ def tile_slstmcell_pa_kernel(
                 raw_tiles["first"] = halves
                 for b in range(2):
                     for u in range(2):
-                        nc.sync.dma_start(
-                            out=halves[:, b, 2 * u : 2 * u + 2, :],
+                        later(nc.sync.dma_start, out=halves[:, b, 2 * u : 2 * u + 2, :],
                             in_=weights[0][0][256 * u : 256 * u + 256, 512 * b : 512 * b + 512].rearrange(
                                 "(p e) n -> p e n", e=2
                             ),
@@ -96,20 +118,18 @@ def tile_slstmcell_pa_kernel(
             if kind == "w":
                 w = weights[g][c // 2]
                 r0 = 512 * (c % 2)
-                nc.sync.dma_start(
-                    out=raw[:].rearrange("p (u e) n -> p u e n", u=2),
+                later(nc.sync.dma_start, out=raw[:].rearrange("p (u e) n -> p u e n", u=2),
                     in_=w[r0 : r0 + 512, :].rearrange("(u p e) n -> p u e n", u=2, e=2),
                 )
             else:
                 src = x if g == 0 else h_prev
-                nc.sync.dma_start(out=raw[:], in_=src.rearrange("(p a) k -> p a k", a=4))
+                later(nc.sync.dma_start, out=raw[:], in_=src.rearrange("(p a) k -> p a k", a=4))
 
         for k in range(RAW_SLOTS):
             issue_next_load()
             if k == 1:
                 for g in range(3):
-                    nc.sync.dma_start(
-                        out=bias_rows[8 * g : 8 * g + 8, :],
+                    later(nc.sync.dma_start, out=bias_rows[8 * g : 8 * g + 8, :],
                         in_=biases[g].rearrange("(m c) -> m c", c=P),
                     )
 
@@ -117,9 +137,9 @@ def tile_slstmcell_pa_kernel(
             o = dst.rearrange("p (c i) t -> p c t i", i=4)
             s = src.rearrange("p t (c i) -> p c t i", i=4)
             if eng == "v":
-                nc.vector.tensor_copy(out=o, in_=s)
+                later(nc.vector.tensor_copy, out=o, in_=s)
             else:
-                nc.scalar.copy(out=o, in_=s)
+                later(nc.scalar.copy, out=o, in_=s)
 
         grps = {}
 
@@ -136,8 +156,7 @@ def tile_slstmcell_pa_kernel(
 
         def q_unit(g, u):
             c, c0 = u // 2, 512 * (u % 2)
-            nc.vector.quantize_mx(
-                out=codes[4 * g + c][:, c0 : c0 + 512].bitcast(FP8X4),
+            later(nc.vector.quantize_mx, out=codes[4 * g + c][:, c0 : c0 + 512].bitcast(FP8X4),
                 scales=planes[4 * g + c][:, c0 : c0 + 512],
                 in_=grps[(g, u)][:].rearrange("p w t -> p (w t)"),
             )
@@ -155,8 +174,7 @@ def tile_slstmcell_pa_kernel(
 
         def q_ztile(m):
             c0 = 512 * (m % 2)
-            nc.vector.quantize_mx(
-                out=codes[8 + m // 2][:, c0 : c0 + 512].bitcast(FP8X4),
+            later(nc.vector.quantize_mx, out=codes[8 + m // 2][:, c0 : c0 + 512].bitcast(FP8X4),
                 scales=planes[8 + m // 2][:, c0 : c0 + 512],
                 in_=grps[(GZ, m)][:].rearrange("p w t -> p (w t)"),
             )
@@ -178,22 +196,19 @@ def tile_slstmcell_pa_kernel(
             for a in range(2):
                 for u in range(2):
                     w0 = 256 * g + 128 * u
-                    nc.tensor.transpose(
-                        bank[:, a, u, :], words[:, 2 * half + a, w0 : w0 + 128], ident32[:]
+                    later(nc.tensor.transpose, out=bank[:, a, u, :], in_=words[:, 2 * half + a, w0 : w0 + 128], identity=ident32[:]
                     )
 
         def xc(s, g, half):
             if half == 0:
                 gxs[(s, g)] = gxp.tile([P, 512, 4], BF16, tag="gx", name="gx_%d_%d" % (s, g), align_bytes=64)
             gx32 = gxs[(s, g)][:].bitcast(F32)
-            nc.scalar.copy(
-                out=gx32[:, 256 * half : 256 * half + 256, :].rearrange("p (a b) u -> p a b u", a=2),
+            later(nc.scalar.copy, out=gx32[:, 256 * half : 256 * half + 256, :].rearrange("p (a b) u -> p a b u", a=2),
                 in_=banks[(s, g, half)][:].rearrange("p a u b -> p a b u"),
             )
 
         def xq(s, g):
-            nc.vector.quantize_mx(
-                out=xcodes[2 * s + g][:].bitcast(FP8X4),
+            later(nc.vector.quantize_mx, out=xcodes[2 * s + g][:].bitcast(FP8X4),
                 scales=xplanes[2 * s + g][:],
                 in_=gxs[(s, g)][:].rearrange("p w t -> p (w t)"),
             )
@@ -205,8 +220,7 @@ def tile_slstmcell_pa_kernel(
                 pl = pool or accp
                 accs[(g, m)] = pl.tile([P, 512], F32, tag="bank", name="acc_%d_%d" % (g, m))
             lhsT, lhsT_scale = stationary(g, m, c)
-            nc.tensor.matmul_mx(
-                out=accs[(g, m)][:],
+            later(nc.tensor.matmul_mx, out=accs[(g, m)][:],
                 lhsT=lhsT,
                 lhsT_scale=lhsT_scale,
                 rhs=xcodes[c][:].bitcast(FP8X4),
@@ -227,8 +241,7 @@ def tile_slstmcell_pa_kernel(
             else:
                 dst = gatep.tile([P, 512], F32, tag="g%d" % g, name="gate_%d_%d" % (g, m))
             sb[(g, m)] = dst
-            nc.scalar.activation(
-                out=dst[:],
+            later(nc.scalar.activation, out=dst[:],
                 in_=accs[(g, m)][:],
                 func=(ACT.Tanh if g == GZ else ACT.Exp),
                 bias=bias_sb[:, 8 * g + m : 8 * g + m + 1],
@@ -242,7 +255,7 @@ def tile_slstmcell_pa_kernel(
             flipped[key] = bank
             src = sb[key]
             for a in range(4):
-                nc.tensor.transpose(bank[:, a, :], src[:, P * a : P * a + P], ident32[:])
+                later(nc.tensor.transpose, out=bank[:, a, :], in_=src[:, P * a : P * a + P], identity=ident32[:])
 
         def part(m):
             for j, grp in enumerate(STORES):
@@ -254,31 +267,28 @@ def tile_slstmcell_pa_kernel(
             for j, grp in enumerate(STORES):
                 if m == grp[-1]:
                     dram = (out_c, out_n)[which]
-                    nc.sync.dma_start(out=dram[:, :, P * grp[0] : P * grp[-1] + P], in_=cn_out[j][:, which])
+                    later(nc.sync.dma_start, out=dram[:, :, P * grp[0] : P * grp[-1] + P], in_=cn_out[j][:, which])
 
         def v_fc_fn(m):
             fT = flipped[(GF, m)]
-            nc.vector.tensor_tensor(
-                out=part(m),
+            later(nc.vector.tensor_tensor, out=part(m),
                 in0=fT[:].unsqueeze(1).to_broadcast([P, 2, 4, P]),
                 in1=cn_sb[:, :, :, P * m : P * m + P],
                 op=ALU.mult,
             )
 
         def v_n(m):
-            nc.vector.tensor_tensor(
-                out=part(m)[:, 1], in0=flipped[(GI, m)][:], in1=part(m)[:, 1], op=ALU.add
+            later(nc.vector.tensor_tensor, out=part(m)[:, 1], in0=flipped[(GI, m)][:], in1=part(m)[:, 1], op=ALU.add
             )
             store_if_full(1, m)
 
         def v_iz(m):
             iz = gatep.tile([P, 512], F32, tag="iz", name="iz%d" % m)
             sb[("iz", m)] = iz
-            nc.vector.tensor_tensor(out=iz[:], in0=i_sb[m][:], in1=sb[(GZ, m)][:], op=ALU.mult)
+            later(nc.vector.tensor_tensor, out=iz[:], in0=i_sb[m][:], in1=sb[(GZ, m)][:], op=ALU.mult)
 
         def v_c(m):
-            nc.vector.tensor_tensor(
-                out=part(m)[:, 0], in0=flipped[("iz", m)][:], in1=part(m)[:, 0], op=ALU.add
+            later(nc.vector.tensor_tensor, out=part(m)[:, 0], in0=flipped[("iz", m)][:], in1=part(m)[:, 0], op=ALU.add
             )
             store_if_full(0, m)
 
@@ -301,8 +311,8 @@ def tile_slstmcell_pa_kernel(
         xq(0, 1)
         first_half_passes(GF, 0)
         bias_ps = trp.tile([P, P], BF16, tag="bank")
-        nc.tensor.transpose(bias_ps[:], bias_rows[:], ident16[:])
-        nc.vector.tensor_copy(out=bias_sb[:], in_=bias_ps[:, 0:24])
+        later(nc.tensor.transpose, out=bias_ps[:], in_=bias_rows[:], identity=ident16[:])
+        later(nc.vector.tensor_copy, out=bias_sb[:], in_=bias_ps[:, 0:24])
         rg_unit(GF, 3, V_COLS_F)
         issue_next_load()
         q_unit(GF, 2)
@@ -369,3 +379,7 @@ def tile_slstmcell_pa_kernel(
                 mx(GI, s + 3)
             v_n(s)
             v_c(s)
+
+        for n in ORDER or range(len(ops)):
+            fn, kw = ops[n]
+            fn(**kw)

@@ -15,29 +15,13 @@ ALU = mybir.AluOpType
 
 P = 128
 RAW_SLOTS = 6
-PINNED = True
-ORDER = (0, 1, 2, 3, 4, 5, 6, 7, 8, 9, 10, 13, 14, 11, 12, 15, 16, 18, 42, 17, 39, 19, 40, 20,
-    21, 22, 24, 25, 26, 27, 29, 23, 30, 31, 32, 34, 35, 36, 37, 28, 51, 41, 33, 52, 43, 38, 44, 45,
-    47, 46, 48, 49, 53, 54, 50, 57, 56, 58, 59, 60, 62, 63, 64, 65, 55, 67, 61, 82, 68, 69, 70, 72,
-    73, 74, 75, 66, 78, 77, 79, 71, 80, 83, 81, 76, 114, 84, 115, 85, 127, 86, 128, 87, 88, 90, 96, 89,
-    95, 91, 97, 92, 99, 93, 98, 94, 116, 107, 101, 129, 100, 106, 102, 109, 119, 103, 104, 118, 105, 122, 117, 130,
-    108, 120, 139, 121, 131, 110, 111, 138, 112, 113, 123, 124, 125, 126, 132, 135, 152, 133, 169, 134, 148, 137, 144, 145,
-    146, 147, 136, 140, 150, 141, 149, 142, 143, 154, 155, 156, 157, 153, 166, 168, 151, 162, 163, 164, 167, 165, 177, 171,
-    170, 172, 173, 174, 175, 178, 176, 190, 180, 181, 179, 182, 183, 158, 188, 159, 160, 191, 161, 184, 199, 185, 189, 186,
-    187, 192, 193, 194, 195, 197, 196, 200, 211, 198, 202, 212, 203, 204, 205, 201, 213, 210, 217, 206, 207, 218, 208, 215,
-    209, 226, 214, 216, 236, 273, 274, 219, 237, 275, 220, 222, 238, 221, 223, 224, 241, 225, 276, 231, 258, 301, 302, 239,
-    240, 303, 253, 232, 259, 233, 260, 234, 242, 263, 235, 254, 255, 286, 261, 256, 281, 257, 262, 304, 289, 327, 287, 328,
-    314, 282, 264, 283, 288, 284, 315, 285, 290, 343, 329, 330, 307, 291, 227, 228, 229, 230, 292, 243, 244, 312, 245, 246,
-    355, 251, 313, 308, 309, 310, 316, 252, 311, 356, 317, 335, 357, 358, 318, 340, 247, 248, 249, 250, 265, 266, 341, 267,
-    368, 268, 336, 277, 342, 337, 338, 279, 339, 344, 278, 269, 270, 271, 272, 345, 361, 293, 280, 294, 295, 296, 305, 366,
-    362, 367, 306, 363, 364, 370, 365, 346, 297, 298, 371, 299, 300, 369, 319, 320, 321, 322, 372, 390, 331, 391, 333, 323,
-    332, 324, 325, 326, 385, 347, 334, 348, 349, 350, 359, 386, 360, 387, 388, 389, 392, 351, 352, 353, 354, 405, 373, 374,
-    375, 376, 381, 383, 377, 382, 378, 379, 380, 406, 393, 384, 394, 395, 396, 401, 403, 397, 402, 398, 399, 400, 411, 407,
-    404, 408, 409, 410, 413, 412, 414)
+PINNED = False
 V_COLS_F = 288
 V_COLS_I = 192
 Z_V_CHUNKS = (1, 2, 1, 2, 1, 2, 1, 2)
 STORES = ((0, 1), (2, 3), (4, 5), (6,), (7,))
+F_BUFS = 8
+LOOK = 2
 GF, GI, GZ = 0, 1, 2
 
 
@@ -53,21 +37,17 @@ def tile_slstmcell_pa_kernel(
         rawp = ctx.enter_context(tc.tile_pool(name="rawp", bufs=RAW_SLOTS))
         grpp = ctx.enter_context(tc.tile_pool(name="grpp", bufs=4))
         gxp = ctx.enter_context(tc.tile_pool(name="gxp", bufs=2))
-        gatep = ctx.enter_context(tc.tile_pool(name="gatep", bufs=3))
-        accp = ctx.enter_context(tc.psum_pool(name="accp", bufs=4))
-        trp = ctx.enter_context(tc.psum_pool(name="trp", bufs=2))
-        flexp = ctx.enter_context(tc.psum_pool(name="flexp", bufs=2))
-
-        ops = []
-
-        def later(fn, **kw):
-            ops.append((fn, kw))
+        gatep = ctx.enter_context(tc.tile_pool(name="gatep", bufs=2))
+        accp = ctx.enter_context(tc.psum_pool(name="psum", bufs=8))
+        trp = accp
+        flexp = accp
+        fpool = ctx.enter_context(tc.tile_pool(name="fpool", bufs=F_BUFS))
 
         weights = ((W_f, U_f), (W_i, U_i), (W_z, U_z))
         biases = (b_f, b_i, b_z)
 
         bias_rows = const.tile([P, P], BF16)
-        later(nc.vector.memset, ap=bias_rows[:], constant=0.0)
+        nc.vector.memset(bias_rows[:], 0.0)
         ident32 = const.tile([P, P], F32)
         make_identity(nc, ident32[:])
         ident16 = const.tile([P, P], BF16)
@@ -99,7 +79,7 @@ def tile_slstmcell_pa_kernel(
             kind, g, c = load_order[k]
             if kind == "c":
                 src = (c_prev, n_prev)[g]
-                later(nc.sync.dma_start, out=cn_sb[:, g], in_=src.rearrange("(p a) h -> p a h", a=4))
+                nc.sync.dma_start(out=cn_sb[:, g], in_=src.rearrange("(p a) h -> p a h", a=4))
                 issue_next_load()
                 return
             if k == 0:
@@ -107,7 +87,8 @@ def tile_slstmcell_pa_kernel(
                 raw_tiles["first"] = halves
                 for b in range(2):
                     for u in range(2):
-                        later(nc.sync.dma_start, out=halves[:, b, 2 * u : 2 * u + 2, :],
+                        nc.sync.dma_start(
+                            out=halves[:, b, 2 * u : 2 * u + 2, :],
                             in_=weights[0][0][256 * u : 256 * u + 256, 512 * b : 512 * b + 512].rearrange(
                                 "(p e) n -> p e n", e=2
                             ),
@@ -118,18 +99,20 @@ def tile_slstmcell_pa_kernel(
             if kind == "w":
                 w = weights[g][c // 2]
                 r0 = 512 * (c % 2)
-                later(nc.sync.dma_start, out=raw[:].rearrange("p (u e) n -> p u e n", u=2),
+                nc.sync.dma_start(
+                    out=raw[:].rearrange("p (u e) n -> p u e n", u=2),
                     in_=w[r0 : r0 + 512, :].rearrange("(u p e) n -> p u e n", u=2, e=2),
                 )
             else:
                 src = x if g == 0 else h_prev
-                later(nc.sync.dma_start, out=raw[:], in_=src.rearrange("(p a) k -> p a k", a=4))
+                nc.sync.dma_start(out=raw[:], in_=src.rearrange("(p a) k -> p a k", a=4))
 
         for k in range(RAW_SLOTS):
             issue_next_load()
             if k == 1:
                 for g in range(3):
-                    later(nc.sync.dma_start, out=bias_rows[8 * g : 8 * g + 8, :],
+                    nc.sync.dma_start(
+                        out=bias_rows[8 * g : 8 * g + 8, :],
                         in_=biases[g].rearrange("(m c) -> m c", c=P),
                     )
 
@@ -137,9 +120,9 @@ def tile_slstmcell_pa_kernel(
             o = dst.rearrange("p (c i) t -> p c t i", i=4)
             s = src.rearrange("p t (c i) -> p c t i", i=4)
             if eng == "v":
-                later(nc.vector.tensor_copy, out=o, in_=s)
+                nc.vector.tensor_copy(out=o, in_=s)
             else:
-                later(nc.scalar.copy, out=o, in_=s)
+                nc.scalar.copy(out=o, in_=s)
 
         grps = {}
 
@@ -156,7 +139,8 @@ def tile_slstmcell_pa_kernel(
 
         def q_unit(g, u):
             c, c0 = u // 2, 512 * (u % 2)
-            later(nc.vector.quantize_mx, out=codes[4 * g + c][:, c0 : c0 + 512].bitcast(FP8X4),
+            nc.vector.quantize_mx(
+                out=codes[4 * g + c][:, c0 : c0 + 512].bitcast(FP8X4),
                 scales=planes[4 * g + c][:, c0 : c0 + 512],
                 in_=grps[(g, u)][:].rearrange("p w t -> p (w t)"),
             )
@@ -174,7 +158,8 @@ def tile_slstmcell_pa_kernel(
 
         def q_ztile(m):
             c0 = 512 * (m % 2)
-            later(nc.vector.quantize_mx, out=codes[8 + m // 2][:, c0 : c0 + 512].bitcast(FP8X4),
+            nc.vector.quantize_mx(
+                out=codes[8 + m // 2][:, c0 : c0 + 512].bitcast(FP8X4),
                 scales=planes[8 + m // 2][:, c0 : c0 + 512],
                 in_=grps[(GZ, m)][:].rearrange("p w t -> p (w t)"),
             )
@@ -196,19 +181,22 @@ def tile_slstmcell_pa_kernel(
             for a in range(2):
                 for u in range(2):
                     w0 = 256 * g + 128 * u
-                    later(nc.tensor.transpose, out=bank[:, a, u, :], in_=words[:, 2 * half + a, w0 : w0 + 128], identity=ident32[:]
+                    nc.tensor.transpose(
+                        bank[:, a, u, :], words[:, 2 * half + a, w0 : w0 + 128], ident32[:]
                     )
 
         def xc(s, g, half):
             if half == 0:
                 gxs[(s, g)] = gxp.tile([P, 512, 4], BF16, tag="gx", name="gx_%d_%d" % (s, g), align_bytes=64)
             gx32 = gxs[(s, g)][:].bitcast(F32)
-            later(nc.scalar.copy, out=gx32[:, 256 * half : 256 * half + 256, :].rearrange("p (a b) u -> p a b u", a=2),
+            nc.scalar.copy(
+                out=gx32[:, 256 * half : 256 * half + 256, :].rearrange("p (a b) u -> p a b u", a=2),
                 in_=banks[(s, g, half)][:].rearrange("p a u b -> p a b u"),
             )
 
         def xq(s, g):
-            later(nc.vector.quantize_mx, out=xcodes[2 * s + g][:].bitcast(FP8X4),
+            nc.vector.quantize_mx(
+                out=xcodes[2 * s + g][:].bitcast(FP8X4),
                 scales=xplanes[2 * s + g][:],
                 in_=gxs[(s, g)][:].rearrange("p w t -> p (w t)"),
             )
@@ -220,7 +208,8 @@ def tile_slstmcell_pa_kernel(
                 pl = pool or accp
                 accs[(g, m)] = pl.tile([P, 512], F32, tag="bank", name="acc_%d_%d" % (g, m))
             lhsT, lhsT_scale = stationary(g, m, c)
-            later(nc.tensor.matmul_mx, out=accs[(g, m)][:],
+            nc.tensor.matmul_mx(
+                out=accs[(g, m)][:],
                 lhsT=lhsT,
                 lhsT_scale=lhsT_scale,
                 rhs=xcodes[c][:].bitcast(FP8X4),
@@ -239,9 +228,10 @@ def tile_slstmcell_pa_kernel(
             if g == GI:
                 dst = i_sb[m]
             else:
-                dst = gatep.tile([P, 512], F32, tag="g%d" % g, name="gate_%d_%d" % (g, m))
+                dst = (fpool if g == GF else gatep).tile([P, 512], F32, tag="g%d" % g, name="gate_%d_%d" % (g, m))
             sb[(g, m)] = dst
-            later(nc.scalar.activation, out=dst[:],
+            nc.scalar.activation(
+                out=dst[:],
                 in_=accs[(g, m)][:],
                 func=(ACT.Tanh if g == GZ else ACT.Exp),
                 bias=bias_sb[:, 8 * g + m : 8 * g + m + 1],
@@ -255,7 +245,7 @@ def tile_slstmcell_pa_kernel(
             flipped[key] = bank
             src = sb[key]
             for a in range(4):
-                later(nc.tensor.transpose, out=bank[:, a, :], in_=src[:, P * a : P * a + P], identity=ident32[:])
+                nc.tensor.transpose(bank[:, a, :], src[:, P * a : P * a + P], ident32[:])
 
         def part(m):
             for j, grp in enumerate(STORES):
@@ -267,35 +257,39 @@ def tile_slstmcell_pa_kernel(
             for j, grp in enumerate(STORES):
                 if m == grp[-1]:
                     dram = (out_c, out_n)[which]
-                    later(nc.sync.dma_start, out=dram[:, :, P * grp[0] : P * grp[-1] + P], in_=cn_out[j][:, which])
+                    nc.sync.dma_start(out=dram[:, :, P * grp[0] : P * grp[-1] + P], in_=cn_out[j][:, which])
 
         def v_fc_fn(m):
             fT = flipped[(GF, m)]
-            later(nc.vector.tensor_tensor, out=part(m),
+            nc.vector.tensor_tensor(
+                out=part(m),
                 in0=fT[:].unsqueeze(1).to_broadcast([P, 2, 4, P]),
                 in1=cn_sb[:, :, :, P * m : P * m + P],
                 op=ALU.mult,
             )
 
         def v_n(m):
-            later(nc.vector.tensor_tensor, out=part(m)[:, 1], in0=flipped[(GI, m)][:], in1=part(m)[:, 1], op=ALU.add
+            nc.vector.tensor_tensor(
+                out=part(m)[:, 1], in0=flipped[(GI, m)][:], in1=part(m)[:, 1], op=ALU.add
             )
             store_if_full(1, m)
 
         def v_iz(m):
             iz = gatep.tile([P, 512], F32, tag="iz", name="iz%d" % m)
             sb[("iz", m)] = iz
-            later(nc.vector.tensor_tensor, out=iz[:], in0=i_sb[m][:], in1=sb[(GZ, m)][:], op=ALU.mult)
+            nc.vector.tensor_tensor(out=iz[:], in0=i_sb[m][:], in1=sb[(GZ, m)][:], op=ALU.mult)
 
         def v_c(m):
-            later(nc.vector.tensor_tensor, out=part(m)[:, 0], in0=flipped[("iz", m)][:], in1=part(m)[:, 0], op=ALU.add
+            nc.vector.tensor_tensor(
+                out=part(m)[:, 0], in0=flipped[("iz", m)][:], in1=part(m)[:, 0], op=ALU.add
             )
             store_if_full(0, m)
 
-        def first_half_passes(g, c):
-            for m in range(4):
+        def passes(g, c, tiles):
+            for m in tiles:
                 mx_pass(g, m, c)
 
+        LO, HI = (0, 1, 2, 3), (4, 5, 6, 7)
         rg_unit(GF, 0, V_COLS_F)
         rg_unit(GF, 1, V_COLS_F)
         issue_next_load()
@@ -309,10 +303,7 @@ def tile_slstmcell_pa_kernel(
         xq(0, 0)
         rg_unit(GF, 2, V_COLS_F)
         xq(0, 1)
-        first_half_passes(GF, 0)
-        bias_ps = trp.tile([P, P], BF16, tag="bank")
-        later(nc.tensor.transpose, out=bias_ps[:], in_=bias_rows[:], identity=ident16[:])
-        later(nc.vector.tensor_copy, out=bias_sb[:], in_=bias_ps[:, 0:24])
+        passes(GF, 0, LO)
         rg_unit(GF, 3, V_COLS_F)
         issue_next_load()
         q_unit(GF, 2)
@@ -321,53 +312,68 @@ def tile_slstmcell_pa_kernel(
                 xt(1, g, half)
                 xc(1, g, half)
         issue_next_load()
-        first_half_passes(GF, 1)
+        passes(GF, 1, LO)
         q_unit(GF, 3)
         xq(1, 0)
         rg_unit(GF, 4, V_COLS_F)
         xq(1, 1)
+        bias_ps = trp.tile([P, P], BF16, tag="bank")
+        nc.tensor.transpose(bias_ps[:], bias_rows[:], ident16[:])
+        nc.vector.tensor_copy(out=bias_sb[:], in_=bias_ps[:, 0:24])
+        passes(GF, 0, HI)
+        passes(GF, 1, HI)
         rg_unit(GF, 5, V_COLS_F)
         issue_next_load()
         q_unit(GF, 4)
-        first_half_passes(GF, 2)
+        passes(GF, 2, LO)
         rg_unit(GF, 6, V_COLS_F)
         q_unit(GF, 5)
+        passes(GF, 2, HI)
         rg_unit(GF, 7, V_COLS_F)
         issue_next_load()
         q_unit(GF, 6)
-        first_half_passes(GF, 3)
+        passes(GF, 3, LO)
 
+        EARLY, LATE = (0, 1, 2, 3, 4, 5), (6, 7)
         for s in range(8):
             rg_unit(GI, s, V_COLS_I)
             if s % 2 == 1:
                 issue_next_load()
-            gate_act(GF, s)
             if s == 0:
                 q_unit(GF, 7)
+                passes(GF, 3, HI)
             else:
                 q_unit(GI, s - 1)
-            flip((GF, s))
+                passes(GI, (s - 1) // 2, [m for m in (LO, HI)[(s - 1) % 2] if m in EARLY])
             if s < 4:
-                mx(GF, s + 4, flexp)
-            if s % 2 == 1:
-                first_half_passes(GI, s // 2)
-            if s > 0:
-                v_fc_fn(s - 1)
+                for m in (2 * s, 2 * s + 1):
+                    gate_act(GF, m)
+                    flip((GF, m))
+            if 0 < s < 5:
+                v_fc_fn(2 * s - 2)
+                v_fc_fn(2 * s - 1)
+            if s == 5:
+                passes(GI, 0, LATE)
+                passes(GI, 1, LATE)
+            if s == 6:
+                passes(GI, 2, LATE)
 
-        rg_ztile(0, Z_V_CHUNKS[0])
-        q_unit(GI, 7)
-        q_ztile(0)
-        rg_ztile(1, Z_V_CHUNKS[1])
-        v_fc_fn(7)
-        mx(GZ, 0, flexp)
+        for m in range(LOOK + 1):
+            rg_ztile(m, Z_V_CHUNKS[m])
+            if m == 0:
+                q_unit(GI, 7)
+                passes(GI, 3, HI)
+        for m in range(LOOK):
+            q_ztile(m)
+            mx(GZ, m)
         gate_act(GI, 0)
         flip((GI, 0))
         for s in range(8):
-            if s < 7:
-                q_ztile(s + 1)
-                mx(GZ, s + 1, flexp)
-            if s < 6:
-                rg_ztile(s + 2, Z_V_CHUNKS[s + 2])
+            if s + LOOK < 8:
+                q_ztile(s + LOOK)
+                mx(GZ, s + LOOK)
+            if s + LOOK + 1 < 8:
+                rg_ztile(s + LOOK + 1, Z_V_CHUNKS[s + LOOK + 1])
             gate_act(GZ, s)
             if s < 7:
                 gate_act(GI, s + 1)
@@ -375,11 +381,5 @@ def tile_slstmcell_pa_kernel(
             flip(("iz", s))
             if s < 7:
                 flip((GI, s + 1))
-            if 4 <= s + 3 < 8:
-                mx(GI, s + 3)
             v_n(s)
             v_c(s)
-
-        for n in ORDER or range(len(ops)):
-            fn, kw = ops[n]
-            fn(**kw)

from contextlib import ExitStack

import concourse.mybir as mybir
from concourse.masks import make_identity

FLOPS = 6 * 2 * 512 * 1024 * 1024

BF16 = mybir.dt.bfloat16
F32 = mybir.dt.float32
U32 = mybir.dt.uint32
U8 = mybir.dt.uint8
FP8X4 = mybir.dt.float8_e4m3fn_x4
ACT = mybir.ActivationFunctionType
ALU = mybir.AluOpType

P = 128
RAW_SLOTS = 6
PINNED = False
V_COLS_F = 288
V_COLS_I = 192
Z_V_CHUNKS = (1, 2, 1, 2, 1, 2, 1, 2)
STORES = ((0, 1), (2, 3), (4, 5), (6,), (7,))
F_BUFS = 8
LOOK = 2
GF, GI, GZ = 0, 1, 2


def tile_slstmcell_pa_kernel(
    tc, x, h_prev, c_prev, n_prev, W_i, b_i, U_i, W_f, b_f, U_f, W_z, b_z, U_z, out_0, out_1
):
    nc = tc.nc
    with ExitStack() as ctx:
        if PINNED:
            ctx.enter_context(tc.manual_schedule())
        const = ctx.enter_context(tc.tile_pool(name="const", bufs=1))
        keep = ctx.enter_context(tc.tile_pool(name="keep", bufs=1))
        rawp = ctx.enter_context(tc.tile_pool(name="rawp", bufs=RAW_SLOTS))
        grpp = ctx.enter_context(tc.tile_pool(name="grpp", bufs=4))
        gxp = ctx.enter_context(tc.tile_pool(name="gxp", bufs=2))
        gatep = ctx.enter_context(tc.tile_pool(name="gatep", bufs=2))
        accp = ctx.enter_context(tc.psum_pool(name="psum", bufs=8))
        trp = accp
        flexp = accp
        fpool = ctx.enter_context(tc.tile_pool(name="fpool", bufs=F_BUFS))

        weights = ((W_f, U_f), (W_i, U_i), (W_z, U_z))
        biases = (b_f, b_i, b_z)

        bias_rows = const.tile([P, P], BF16)
        nc.vector.memset(bias_rows[:], 0.0)
        ident32 = const.tile([P, P], F32)
        make_identity(nc, ident32[:])
        ident16 = const.tile([P, P], BF16)
        make_identity(nc, ident16[:])
        bias_sb = const.tile([P, 24], F32)

        codes = [keep.tile([P, 1024], U32, name="codes%d" % c, align_bytes=64) for c in range(12)]
        planes = [keep.tile([P, 1024], U8, name="planes%d" % c, align_bytes=64) for c in range(12)]
        xcodes = [keep.tile([P, 512], U32, name="xcodes%d" % c, align_bytes=64) for c in range(4)]
        xplanes = [keep.tile([P, 512], U8, name="xplanes%d" % c, align_bytes=64) for c in range(4)]
        cn_sb = keep.tile([P, 2, 4, 1024], BF16)
        i_sb = [keep.tile([P, 512], F32, name="i_sb%d" % m) for m in range(8)]
        cn_out = [keep.tile([P, 2, 4, P * len(grp)], F32, name="cn_out%d" % grp[0]) for grp in STORES]

        out_c = out_0.rearrange("(p a) h -> p a h", a=4)
        out_n = out_1.rearrange("(p a) h -> p a h", a=4)

        load_order = [("w", 0, 0), ("a", 0, 0), ("w", 0, 1), ("a", 1, 0), ("w", 0, 2), ("w", 0, 3)]
        load_order += [("w", 1, 0), ("c", 0, 0), ("c", 1, 0), ("w", 1, 1), ("w", 1, 2), ("w", 1, 3)]
        load_order += [("w", 2, c) for c in range(4)]
        raw_tiles = {}
        state = {"load": 0}

        def issue_next_load():
            k = state["load"]
            if k >= len(load_order):
                return
            state["load"] = k + 1
            kind, g, c = load_order[k]
            if kind == "c":
                src = (c_prev, n_prev)[g]
                nc.sync.dma_start(out=cn_sb[:, g], in_=src.rearrange("(p a) h -> p a h", a=4))
                issue_next_load()
                return
            if k == 0:
                halves = rawp.tile([P, 2, 4, 512], BF16, tag="raw")
                raw_tiles["first"] = halves
                for b in range(2):
                    for u in range(2):
                        nc.sync.dma_start(
                            out=halves[:, b, 2 * u : 2 * u + 2, :],
                            in_=weights[0][0][256 * u : 256 * u + 256, 512 * b : 512 * b + 512].rearrange(
                                "(p e) n -> p e n", e=2
                            ),
                        )
                return
            raw = rawp.tile([P, 4, 1024], BF16, tag="raw", name="raw%d" % k)
            raw_tiles[load_order[k]] = raw
            if kind == "w":
                w = weights[g][c // 2]
                r0 = 512 * (c % 2)
                nc.sync.dma_start(
                    out=raw[:].rearrange("p (u e) n -> p u e n", u=2),
                    in_=w[r0 : r0 + 512, :].rearrange("(u p e) n -> p u e n", u=2, e=2),
                )
            else:
                src = x if g == 0 else h_prev
                nc.sync.dma_start(out=raw[:], in_=src.rearrange("(p a) k -> p a k", a=4))

        for k in range(RAW_SLOTS):
            issue_next_load()
            if k == 1:
                for g in range(3):
                    nc.sync.dma_start(
                        out=bias_rows[8 * g : 8 * g + 8, :],
                        in_=biases[g].rearrange("(m c) -> m c", c=P),
                    )

        def regroup(eng, dst, src):
            o = dst.rearrange("p (c i) t -> p c t i", i=4)
            s = src.rearrange("p t (c i) -> p c t i", i=4)
            if eng == "v":
                nc.vector.tensor_copy(out=o, in_=s)
            else:
                nc.scalar.copy(out=o, in_=s)

        grps = {}

        def rg_unit(g, u, vcols):
            c, c0 = u // 2, 512 * (u % 2)
            if g == 0 and c == 0:
                src = raw_tiles["first"][:, u]
            else:
                src = raw_tiles[("w", g, c)][:, :, c0 : c0 + 512]
            grp = grpp.tile([P, 512, 4], BF16, tag="grp", name="grp_%d_%d" % (g, u), align_bytes=64)
            grps[(g, u)] = grp
            regroup("v", grp[:, 0:vcols, :], src[:, :, 0:vcols])
            regroup("s", grp[:, vcols:512, :], src[:, :, vcols:512])

        def q_unit(g, u):
            c, c0 = u // 2, 512 * (u % 2)
            nc.vector.quantize_mx(
                out=codes[4 * g + c][:, c0 : c0 + 512].bitcast(FP8X4),
                scales=planes[4 * g + c][:, c0 : c0 + 512],
                in_=grps[(g, u)][:].rearrange("p w t -> p (w t)"),
            )

        def rg_ztile(m, v_chunks):
            grp = grpp.tile([P, 512, 4], BF16, tag="grp", name="grp_z_%d" % m, align_bytes=64)
            grps[(GZ, m)] = grp
            for c in range(4):
                raw = raw_tiles[("w", GZ, c)]
                regroup(
                    "v" if c >= 4 - v_chunks else "s",
                    grp[:, P * c : P * c + P, :],
                    raw[:, :, P * m : P * m + P],
                )

        def q_ztile(m):
            c0 = 512 * (m % 2)
            nc.vector.quantize_mx(
                out=codes[8 + m // 2][:, c0 : c0 + 512].bitcast(FP8X4),
                scales=planes[8 + m // 2][:, c0 : c0 + 512],
                in_=grps[(GZ, m)][:].rearrange("p w t -> p (w t)"),
            )

        def stationary(g, m, c):
            if g == GZ:
                t, c0 = 8 + m // 2, 512 * (m % 2) + P * c
            else:
                t, c0 = 4 * g + c, P * m
            return codes[t][:, c0 : c0 + P].bitcast(FP8X4), planes[t][:, c0 : c0 + P]

        gxs = {}
        banks = {}

        def xt(s, g, half):
            words = raw_tiles[("a", s, 0)][:].bitcast(F32)
            bank = (trp, flexp)[half].tile([P, 2, 2, P], F32, tag="bank", name="xt_%d_%d_%d" % (s, g, half))
            banks[(s, g, half)] = bank
            for a in range(2):
                for u in range(2):
                    w0 = 256 * g + 128 * u
                    nc.tensor.transpose(
                        bank[:, a, u, :], words[:, 2 * half + a, w0 : w0 + 128], ident32[:]
                    )

        def xc(s, g, half):
            if half == 0:
                gxs[(s, g)] = gxp.tile([P, 512, 4], BF16, tag="gx", name="gx_%d_%d" % (s, g), align_bytes=64)
            gx32 = gxs[(s, g)][:].bitcast(F32)
            nc.scalar.copy(
                out=gx32[:, 256 * half : 256 * half + 256, :].rearrange("p (a b) u -> p a b u", a=2),
                in_=banks[(s, g, half)][:].rearrange("p a u b -> p a b u"),
            )

        def xq(s, g):
            nc.vector.quantize_mx(
                out=xcodes[2 * s + g][:].bitcast(FP8X4),
                scales=xplanes[2 * s + g][:],
                in_=gxs[(s, g)][:].rearrange("p w t -> p (w t)"),
            )

        accs = {}

        def mx_pass(g, m, c, pool=None):
            if c == 0:
                pl = pool or accp
                accs[(g, m)] = pl.tile([P, 512], F32, tag="bank", name="acc_%d_%d" % (g, m))
            lhsT, lhsT_scale = stationary(g, m, c)
            nc.tensor.matmul_mx(
                out=accs[(g, m)][:],
                lhsT=lhsT,
                lhsT_scale=lhsT_scale,
                rhs=xcodes[c][:].bitcast(FP8X4),
                rhs_scale=xplanes[c][:],
                start=(c == 0),
                stop=(c == 3),
            )

        def mx(g, m, pool=None):
            for c in range(4):
                mx_pass(g, m, c, pool)

        sb = {}

        def gate_act(g, m):
            if g == GI:
                dst = i_sb[m]
            else:
                dst = (fpool if g == GF else gatep).tile([P, 512], F32, tag="g%d" % g, name="gate_%d_%d" % (g, m))
            sb[(g, m)] = dst
            nc.scalar.activation(
                out=dst[:],
                in_=accs[(g, m)][:],
                func=(ACT.Tanh if g == GZ else ACT.Exp),
                bias=bias_sb[:, 8 * g + m : 8 * g + m + 1],
                scale=1.0,
            )

        flipped = {}

        def flip(key, pool=None):
            bank = (pool or trp).tile([P, 4, P], F32, tag="bank", name="T_%s_%d" % key)
            flipped[key] = bank
            src = sb[key]
            for a in range(4):
                nc.tensor.transpose(bank[:, a, :], src[:, P * a : P * a + P], ident32[:])

        def part(m):
            for j, grp in enumerate(STORES):
                if m in grp:
                    off = P * grp.index(m)
                    return cn_out[j][:, :, :, off : off + P]

        def store_if_full(which, m):
            for j, grp in enumerate(STORES):
                if m == grp[-1]:
                    dram = (out_c, out_n)[which]
                    nc.sync.dma_start(out=dram[:, :, P * grp[0] : P * grp[-1] + P], in_=cn_out[j][:, which])

        def v_fc_fn(m):
            fT = flipped[(GF, m)]
            nc.vector.tensor_tensor(
                out=part(m),
                in0=fT[:].unsqueeze(1).to_broadcast([P, 2, 4, P]),
                in1=cn_sb[:, :, :, P * m : P * m + P],
                op=ALU.mult,
            )

        def v_n(m):
            nc.vector.tensor_tensor(
                out=part(m)[:, 1], in0=flipped[(GI, m)][:], in1=part(m)[:, 1], op=ALU.add
            )
            store_if_full(1, m)

        def v_iz(m):
            iz = gatep.tile([P, 512], F32, tag="iz", name="iz%d" % m)
            sb[("iz", m)] = iz
            nc.vector.tensor_tensor(out=iz[:], in0=i_sb[m][:], in1=sb[(GZ, m)][:], op=ALU.mult)

        def v_c(m):
            nc.vector.tensor_tensor(
                out=part(m)[:, 0], in0=flipped[("iz", m)][:], in1=part(m)[:, 0], op=ALU.add
            )
            store_if_full(0, m)

        def passes(g, c, tiles):
            for m in tiles:
                mx_pass(g, m, c)

        LO, HI = (0, 1, 2, 3), (4, 5, 6, 7)
        rg_unit(GF, 0, V_COLS_F)
        rg_unit(GF, 1, V_COLS_F)
        issue_next_load()
        q_unit(GF, 0)
        for g in range(2):
            for half in range(2):
                xt(0, g, half)
                xc(0, g, half)
        issue_next_load()
        q_unit(GF, 1)
        xq(0, 0)
        rg_unit(GF, 2, V_COLS_F)
        xq(0, 1)
        passes(GF, 0, LO)
        rg_unit(GF, 3, V_COLS_F)
        issue_next_load()
        q_unit(GF, 2)
        for g in range(2):
            for half in range(2):
                xt(1, g, half)
                xc(1, g, half)
        issue_next_load()
        passes(GF, 1, LO)
        q_unit(GF, 3)
        xq(1, 0)
        rg_unit(GF, 4, V_COLS_F)
        xq(1, 1)
        bias_ps = trp.tile([P, P], BF16, tag="bank")
        nc.tensor.transpose(bias_ps[:], bias_rows[:], ident16[:])
        nc.vector.tensor_copy(out=bias_sb[:], in_=bias_ps[:, 0:24])
        passes(GF, 0, HI)
        passes(GF, 1, HI)
        rg_unit(GF, 5, V_COLS_F)
        issue_next_load()
        q_unit(GF, 4)
        passes(GF, 2, LO)
        rg_unit(GF, 6, V_COLS_F)
        q_unit(GF, 5)
        passes(GF, 2, HI)
        rg_unit(GF, 7, V_COLS_F)
        issue_next_load()
        q_unit(GF, 6)
        passes(GF, 3, LO)

        EARLY, LATE = (0, 1, 2, 3, 4, 5), (6, 7)
        for s in range(8):
            rg_unit(GI, s, V_COLS_I)
            if s % 2 == 1:
                issue_next_load()
            if s == 0:
                q_unit(GF, 7)
                passes(GF, 3, HI)
            else:
                q_unit(GI, s - 1)
                passes(GI, (s - 1) // 2, [m for m in (LO, HI)[(s - 1) % 2] if m in EARLY])
            if s < 4:
                for m in (2 * s, 2 * s + 1):
                    gate_act(GF, m)
                    flip((GF, m))
            if 0 < s < 5:
                v_fc_fn(2 * s - 2)
                v_fc_fn(2 * s - 1)
            if s == 5:
                passes(GI, 0, LATE)
                passes(GI, 1, LATE)
            if s == 6:
                passes(GI, 2, LATE)

        for m in range(LOOK + 1):
            rg_ztile(m, Z_V_CHUNKS[m])
            if m == 0:
                q_unit(GI, 7)
                passes(GI, 3, HI)
        for m in range(LOOK):
            q_ztile(m)
            mx(GZ, m)
        gate_act(GI, 0)
        flip((GI, 0))
        for s in range(8):
            if s + LOOK < 8:
                q_ztile(s + LOOK)
                mx(GZ, s + LOOK)
            if s + LOOK + 1 < 8:
                rg_ztile(s + LOOK + 1, Z_V_CHUNKS[s + LOOK + 1])
            gate_act(GZ, s)
            if s < 7:
                gate_act(GI, s + 1)
            v_iz(s)
            flip(("iz", s))
            if s < 7:
                flip((GI, s + 1))
            v_n(s)
            v_c(s)
